import numpy as np
import ml_dtypes


def mxq(x, axis, fmt="e4m3"):
    dtype, down = {"e4m3": (ml_dtypes.float8_e4m3fn, 7), "e5m2": (ml_dtypes.float8_e5m2, 14)}[fmt]
    v = np.moveaxis(np.asarray(x, np.float32).astype(ml_dtypes.bfloat16).astype(np.float64), axis, -1)
    blocks = v.reshape(v.shape[:-1] + (-1, 32))
    amax = np.abs(blocks).max(-1, keepdims=True)
    byte = np.maximum(np.where(amax > 0, np.frexp(amax)[1] - 1 + 127, 0) - down, 1)
    scale = np.exp2(byte - 127.0)
    codes = (blocks / scale).astype(np.float32).astype(dtype).astype(np.float64)
    return np.moveaxis((codes * scale).reshape(v.shape), -1, axis)


WIDE = False


def mx_kscale(k):
    if not WIDE:
        return np.ones(k)
    levels = np.array([10, -10, 5, -5, 0])
    if k % 512:
        return np.exp2(np.random.permutation(np.resize(levels, k // 32))).repeat(32)
    a = np.empty((k // 512, 16))
    for p in range(k // 512):
        a[p, :8] = np.random.permutation(np.resize(levels, 8))
        for g in range(8):
            far = levels[np.abs(levels - a[p, g]) >= 10]
            a[p, g + 8] = far[np.random.randint(len(far))]
    return np.exp2(a.ravel()).repeat(32)


BF16 = ml_dtypes.bfloat16


def bf(x):
    return np.asarray(x, np.float32).astype(BF16)


def f64(x):
    return np.asarray(x).astype(np.float64)


B, D_IN, UNITS = 1024, 512, 512


def sigmoid(v):
    return 1.0 / (1.0 + np.exp(-v))


def setup_inputs():
    s, t = mx_kscale(D_IN), mx_kscale(UNITS)
    sx, sh = 1.0 / np.sqrt(D_IN), 1.0 / np.sqrt(UNITS)
    return {"input_x": bf(np.random.standard_normal((B, D_IN)) * s),
            "input_h": bf(np.random.standard_normal((B, UNITS)) * t),
            "Wx_r": bf(np.random.standard_normal((D_IN, UNITS)) * sx / s[:, None]),
            "b_r": bf(np.random.standard_normal(UNITS) * 0.5),
            "Wh_r": bf(np.random.standard_normal((UNITS, UNITS)) * sh / t[:, None]),
            "Wx_h": bf(np.random.standard_normal((D_IN, UNITS)) * sx / s[:, None]),
            "b_h": bf(np.random.standard_normal(UNITS) * 0.5),
            "Wh_h": bf(np.random.standard_normal((UNITS, UNITS)) * sh / t[:, None])}


def reference(input_x, input_h, Wx_r, b_r, Wh_r, Wx_h, b_h, Wh_h):
    xq = mxq(f64(input_x), 1, "e4m3")
    hq = mxq(f64(input_h), 1, "e4m3")
    r = sigmoid((xq @ mxq(f64(Wx_r), 0, "e4m3")) + f64(b_r) + (hq @ mxq(f64(Wh_r), 0, "e4m3")))
    return np.tanh((xq @ mxq(f64(Wx_h), 0, "e4m3")) + f64(b_h) + r * (hq @ mxq(f64(Wh_h), 0, "e4m3")))

@@ -1,0 +1,213 @@
+from contextlib import ExitStack
+
+import concourse.mybir as mybir
+from concourse.masks import make_identity
+
+F32 = mybir.dt.float32
+BF16 = mybir.dt.bfloat16
+U32 = mybir.dt.uint32
+U8 = mybir.dt.uint8
+FP8X4 = mybir.dt.float8_e4m3fn_x4
+ACT = mybir.ActivationFunctionType
+ALU = mybir.AluOpType
+
+P = 128
+PACK = 4
+K = P * PACK
+BATCH = 1024
+UNITS = 512
+CHUNK = 512
+N_CHUNKS = BATCH // CHUNK
+ROW_TILES = CHUNK // P
+UNIT_TILES = UNITS // P
+WORDS = K // 2
+RUN = 4
+COLUMN_RUNS = UNITS // RUN
+VECTOR_RUNS = 5 * COLUMN_RUNS // 8
+
+FLOPS = 4 * 2 * BATCH * K * UNITS
+
+
+def tile_augru_pa_kernel(
+    tc, input_x, input_h, Wx_r, b_r, Wh_r, Wx_h, b_h, Wh_h, out
+):
+    nc = tc.nc
+    with ExitStack() as ctx:
+        const = ctx.enter_context(tc.tile_pool(name="const", bufs=1))
+        raw = ctx.enter_context(tc.tile_pool(name="raw", bufs=1))
+        mx = ctx.enter_context(tc.tile_pool(name="mx", bufs=1))
+        work = ctx.enter_context(tc.tile_pool(name="work", bufs=N_CHUNKS * UNIT_TILES))
+        banks = ctx.enter_context(tc.psum_pool(name="banks", bufs=8))
+        ctx.enter_context(tc.manual_schedule())
+
+        bias_rows = const.tile([P, P], BF16)
+        nc.gpsimd.memset(bias_rows[:], 0.0)
+        nc.scalar.dma_start(out=bias_rows[0:UNIT_TILES, :], in_=b_r.rearrange("(i n) -> i n", n=P))
+        nc.scalar.dma_start(
+            out=bias_rows[UNIT_TILES : 2 * UNIT_TILES, :], in_=b_h.rearrange("(i n) -> i n", n=P)
+        )
+        warm = const.tile([P, 2], F32)
+        nc.gpsimd.memset(warm[:], 0.0)
+        nc.scalar.activation(out=warm[:, 1:2], in_=warm[:, 0:1], func=ACT.Sigmoid)
+        ident = const.tile([P, P], F32)
+        make_identity(nc, ident[:])
+        bias_square = const.tile([P, P], F32)
+        nc.gpsimd.tensor_copy(out=bias_square[:], in_=bias_rows[:])
+
+        def load_rows(name, rows):
+            tile = raw.tile([P, ROW_TILES * K], BF16, name=name)
+            nc.sync.dma_start(out=tile[:], in_=rows.rearrange("(p t) k -> p (t k)", t=ROW_TILES))
+            return tile
+
+        def load_weight(name, weight):
+            tile = raw.tile([P, PACK, UNITS], BF16, name=name)
+            nc.sync.dma_start(out=tile[:], in_=weight.rearrange("(q j) n -> q j n", j=PACK))
+            return tile
+
+        x_raw = [None] * N_CHUNKS
+        h_raw = [None] * N_CHUNKS
+        x_raw[0] = load_rows("x_raw0", input_x[0:CHUNK, :])
+        h_raw[0] = load_rows("h_raw0", input_h[0:CHUNK, :])
+        wxr_raw = load_weight("wxr_raw", Wx_r)
+        whr_raw = load_weight("whr_raw", Wh_r)
+        x_raw[1] = load_rows("x_raw1", input_x[CHUNK:BATCH, :])
+        h_raw[1] = load_rows("h_raw1", input_h[CHUNK:BATCH, :])
+        whh_raw = load_weight("whh_raw", Wh_h)
+        wxh_raw = load_weight("wxh_raw", Wx_h)
+
+        def transpose_rows(name, rows_raw):
+            grouped = mx.tile([P, CHUNK * PACK], BF16, name=name, align_bytes=64)
+            words = rows_raw[:].bitcast(F32)
+            grouped_words = grouped[:].bitcast(F32).rearrange("q (col u) -> q col u", u=2)
+            for half in range(2):
+                bank = banks.tile([P, CHUNK], F32, tag="bank")
+                planes = bank[:].rearrange("q (u col) -> q u col", u=2)
+                for local in range(2):
+                    first_word = (2 * half + local) * WORDS
+                    for u in range(2):
+                        nc.tensor.transpose(
+                            out=planes[:, u, local * P : (local + 1) * P],
+                            in_=words[:, first_word + u : first_word + WORDS : 2],
+                            identity=ident[:],
+                        )
+                nc.scalar.copy(
+                    out=grouped_words[:, half * 2 * P : (half + 1) * 2 * P, :],
+                    in_=planes.rearrange("q u col -> q col u"),
+                )
+            return grouped[:]
+
+        def regroup_weight(name, weight_raw):
+            grouped = mx.tile([P, UNITS, PACK], BF16, name=name, align_bytes=64)
+            dst = grouped[:].rearrange("q (c i) t -> q c t i", i=RUN)
+            src = weight_raw[:].rearrange("q t (c i) -> q c t i", i=RUN)
+            nc.vector.tensor_copy(out=dst[:, :VECTOR_RUNS], in_=src[:, :VECTOR_RUNS])
+            nc.scalar.copy(out=dst[:, VECTOR_RUNS:], in_=src[:, VECTOR_RUNS:])
+            return grouped[:].rearrange("q n t -> q (n t)")
+
+        def quantise(name, grouped):
+            codes = mx.tile([P, CHUNK], U32, name=name + "_codes", align_bytes=64)
+            scales = mx.tile([P, CHUNK], U8, name=name + "_scales", align_bytes=64)
+            nc.vector.quantize_mx(out=codes[:].bitcast(FP8X4), scales=scales[:], in_=grouped)
+            return codes, scales
+
+        def mx_pass(acc, weight, i, rows, start, stop):
+            units = slice(i * P, (i + 1) * P)
+            nc.tensor.matmul_mx(
+                out=acc[:],
+                lhsT=weight[0][:, units].bitcast(FP8X4),
+                lhsT_scale=weight[1][:, units],
+                rhs=rows[0][:].bitcast(FP8X4),
+                rhs_scale=rows[1][:],
+                start=start,
+                stop=stop,
+            )
+
+        x_mx = [None] * N_CHUNKS
+        h_mx = [None] * N_CHUNKS
+        x_grouped = transpose_rows("x_grouped0", x_raw[0])
+        h_grouped = transpose_rows("h_grouped0", h_raw[0])
+        x_mx[0] = quantise("x0", x_grouped)
+        wxr_grouped = regroup_weight("wxr_grouped", wxr_raw)
+        h_mx[0] = quantise("h0", h_grouped)
+        whr_grouped = regroup_weight("whr_grouped", whr_raw)
+        wxr = quantise("wxr", wxr_grouped)
+        whr = quantise("whr", whr_grouped)
+        x_grouped = transpose_rows("x_grouped1", x_raw[1])
+        whh_grouped = regroup_weight("whh_grouped", whh_raw)
+        x_mx[1] = quantise("x1", x_grouped)
+        whh = quantise("whh", whh_grouped)
+        h_grouped = transpose_rows("h_grouped1", h_raw[1])
+        wxh_grouped = regroup_weight("wxh_grouped", wxh_raw)
+        bias_bank = banks.tile([P, CHUNK], F32, tag="bank")
+        nc.tensor.transpose(out=bias_bank[:, 0:P], in_=bias_square[:], identity=ident[:])
+        bias = const.tile([P, 2 * UNIT_TILES], F32)
+        nc.vector.tensor_copy(out=bias[:], in_=bias_bank[:, 0 : 2 * UNIT_TILES])
+        h_mx[1] = quantise("h1", h_grouped)
+        wxh = quantise("wxh", wxh_grouped)
+
+        gate = [[None] * UNIT_TILES for c in range(N_CHUNKS)]
+        gated = [[None] * UNIT_TILES for c in range(N_CHUNKS)]
+        summed = [[None] * UNIT_TILES for c in range(N_CHUNKS)]
+
+        def reset_gate(c, i):
+            acc = banks.tile([P, CHUNK], F32, tag="bank")
+            mx_pass(acc, wxr, i, x_mx[c], True, False)
+            mx_pass(acc, whr, i, h_mx[c], False, True)
+            r = work.tile([P, CHUNK], F32, tag="gate")
+            nc.scalar.activation(out=r[:], in_=acc[:], func=ACT.Sigmoid, bias=bias[:, i : i + 1])
+            gate[c][i] = r
+
+        def gated_state(c, i):
+            acc = banks.tile([P, CHUNK], F32, tag="bank")
+            mx_pass(acc, whh, i, h_mx[c], True, True)
+            product = work.tile([P, CHUNK], F32, tag="gated")
+            nc.vector.tensor_tensor(out=product[:], in0=gate[c][i][:], in1=acc[:], op=ALU.mult)
+            gated[c][i] = product
+
+        def candidate_sum(c, i):
+            acc = banks.tile([P, CHUNK], F32, tag="bank")
+            mx_pass(acc, wxh, i, x_mx[c], True, True)
+            total = work.tile([P, CHUNK], F32, tag="summed")
+            nc.vector.scalar_tensor_tensor(
+                out=total[:],
+                in0=acc[:],
+                scalar=bias[:, UNIT_TILES + i : UNIT_TILES + i + 1],
+                in1=gated[c][i][:],
+                op0=ALU.add,
+                op1=ALU.add,
+            )
+            summed[c][i] = total
+
+        def finish(c, i):
+            bank = banks.tile([P, CHUNK], F32, tag="bank")
+            for t in range(ROW_TILES):
+                nc.tensor.transpose(
+                    out=bank[:, t * P : (t + 1) * P],
+                    in_=summed[c][i][:, t * P : (t + 1) * P],
+                    identity=ident[:],
+                )
+            result = work.tile([P, CHUNK], F32, tag="result")
+            nc.scalar.activation(out=result[:], in_=bank[:], func=ACT.Tanh)
+            nc.sync.dma_start(
+                out=out[c * CHUNK : (c + 1) * CHUNK, i * P : (i + 1) * P].rearrange(
+                    "(p t) n -> p t n", t=ROW_TILES
+                ),
+                in_=result[:].rearrange("p (t n) -> p t n", t=ROW_TILES),
+            )
+
+        for i in range(UNIT_TILES):
+            reset_gate(0, i)
+        for i in range(UNIT_TILES):
+            gated_state(0, i)
+        for i in range(UNIT_TILES):
+            candidate_sum(0, i)
+        for i in range(UNIT_TILES):
+            reset_gate(1, i)
+        for i in range(UNIT_TILES):
+            gated_state(1, i)
+        for i in range(UNIT_TILES):
+            finish(0, i)
+        for i in range(UNIT_TILES):
+            candidate_sum(1, i)
+        for i in range(UNIT_TILES):
+            finish(1, i)

@@ -16,10 +16,13 @@ PACK = 4
 K = P * PACK
 BATCH = 1024
 UNITS = 512
-CHUNK = 512
+CHUNK = 256
 N_CHUNKS = BATCH // CHUNK
 ROW_TILES = CHUNK // P
 UNIT_TILES = UNITS // P
+PAIR = 2
+PAIRS = UNIT_TILES // PAIR
+BANK = PAIR * CHUNK
 WORDS = K // 2
 RUN = 4
 COLUMN_RUNS = UNITS // RUN
@@ -36,26 +39,21 @@ def tile_augru_pa_kernel(
         const = ctx.enter_context(tc.tile_pool(name="const", bufs=1))
         raw = ctx.enter_context(tc.tile_pool(name="raw", bufs=1))
         mx = ctx.enter_context(tc.tile_pool(name="mx", bufs=1))
-        work = ctx.enter_context(tc.tile_pool(name="work", bufs=N_CHUNKS * UNIT_TILES))
+        work = ctx.enter_context(tc.tile_pool(name="work", bufs=N_CHUNKS * PAIRS))
         banks = ctx.enter_context(tc.psum_pool(name="banks", bufs=8))
         ctx.enter_context(tc.manual_schedule())
 
         bias_rows = const.tile([P, P], BF16)
         nc.gpsimd.memset(bias_rows[:], 0.0)
-        nc.scalar.dma_start(out=bias_rows[0:UNIT_TILES, :], in_=b_r.rearrange("(i n) -> i n", n=P))
-        nc.scalar.dma_start(
-            out=bias_rows[UNIT_TILES : 2 * UNIT_TILES, :], in_=b_h.rearrange("(i n) -> i n", n=P)
-        )
         warm = const.tile([P, 2], F32)
         nc.gpsimd.memset(warm[:], 0.0)
         nc.scalar.activation(out=warm[:, 1:2], in_=warm[:, 0:1], func=ACT.Sigmoid)
         ident = const.tile([P, P], F32)
         make_identity(nc, ident[:])
-        bias_square = const.tile([P, P], F32)
-        nc.gpsimd.tensor_copy(out=bias_square[:], in_=bias_rows[:])
 
-        def load_rows(name, rows):
+        def load_rows(name, tensor, c):
             tile = raw.tile([P, ROW_TILES * K], BF16, name=name)
+            rows = tensor[c * CHUNK : (c + 1) * CHUNK, :]
             nc.sync.dma_start(out=tile[:], in_=rows.rearrange("(p t) k -> p (t k)", t=ROW_TILES))
             return tile
 
@@ -66,34 +64,42 @@ def tile_augru_pa_kernel(
 
         x_raw = [None] * N_CHUNKS
         h_raw = [None] * N_CHUNKS
-        x_raw[0] = load_rows("x_raw0", input_x[0:CHUNK, :])
-        h_raw[0] = load_rows("h_raw0", input_h[0:CHUNK, :])
         wxr_raw = load_weight("wxr_raw", Wx_r)
+        x_raw[0] = load_rows("x_raw0", input_x, 0)
+        h_raw[0] = load_rows("h_raw0", input_h, 0)
+        nc.sync.dma_start(out=bias_rows[0:UNIT_TILES, :], in_=b_r.rearrange("(i n) -> i n", n=P))
+        nc.sync.dma_start(
+            out=bias_rows[UNIT_TILES : 2 * UNIT_TILES, :], in_=b_h.rearrange("(i n) -> i n", n=P)
+        )
         whr_raw = load_weight("whr_raw", Wh_r)
-        x_raw[1] = load_rows("x_raw1", input_x[CHUNK:BATCH, :])
-        h_raw[1] = load_rows("h_raw1", input_h[CHUNK:BATCH, :])
         whh_raw = load_weight("whh_raw", Wh_h)
+        x_raw[1] = load_rows("x_raw1", input_x, 1)
+        h_raw[1] = load_rows("h_raw1", input_h, 1)
         wxh_raw = load_weight("wxh_raw", Wx_h)
+        for c in range(2, N_CHUNKS):
+            x_raw[c] = load_rows("x_raw%d" % c, input_x, c)
+            h_raw[c] = load_rows("h_raw%d" % c, input_h, c)
+        bias_square = const.tile([P, P], F32)
+        nc.gpsimd.tensor_copy(out=bias_square[:], in_=bias_rows[:])
 
-        def transpose_rows(name, rows_raw):
-            grouped = mx.tile([P, CHUNK * PACK], BF16, name=name, align_bytes=64)
+        def transpose_rows(rows_raw):
             words = rows_raw[:].bitcast(F32)
-            grouped_words = grouped[:].bitcast(F32).rearrange("q (col u) -> q col u", u=2)
-            for half in range(2):
-                bank = banks.tile([P, CHUNK], F32, tag="bank")
-                planes = bank[:].rearrange("q (u col) -> q u col", u=2)
-                for local in range(2):
-                    first_word = (2 * half + local) * WORDS
-                    for u in range(2):
-                        nc.tensor.transpose(
-                            out=planes[:, u, local * P : (local + 1) * P],
-                            in_=words[:, first_word + u : first_word + WORDS : 2],
-                            identity=ident[:],
-                        )
-                nc.scalar.copy(
-                    out=grouped_words[:, half * 2 * P : (half + 1) * 2 * P, :],
-                    in_=planes.rearrange("q u col -> q col u"),
-                )
+            bank = banks.tile([P, BANK], F32, tag="bank")
+            for t in range(ROW_TILES):
+                for u in range(2):
+                    nc.tensor.transpose(
+                        out=bank[:, u * CHUNK + t * P : u * CHUNK + (t + 1) * P],
+                        in_=words[:, t * WORDS + u : (t + 1) * WORDS : 2],
+                        identity=ident[:],
+                    )
+            return bank
+
+        def group_rows(name, bank):
+            grouped = mx.tile([P, CHUNK * PACK], BF16, name=name, align_bytes=64)
+            nc.scalar.copy(
+                out=grouped[:].bitcast(F32).rearrange("q (col u) -> q col u", u=2),
+                in_=bank[:].rearrange("q (u col) -> q col u", u=2),
+            )
             return grouped[:]
 
         def regroup_weight(name, weight_raw):
@@ -104,16 +110,16 @@ def tile_augru_pa_kernel(
             nc.scalar.copy(out=dst[:, VECTOR_RUNS:], in_=src[:, VECTOR_RUNS:])
             return grouped[:].rearrange("q n t -> q (n t)")
 
-        def quantise(name, grouped):
-            codes = mx.tile([P, CHUNK], U32, name=name + "_codes", align_bytes=64)
-            scales = mx.tile([P, CHUNK], U8, name=name + "_scales", align_bytes=64)
+        def quantise(name, grouped, columns):
+            codes = mx.tile([P, columns], U32, name=name + "_codes", align_bytes=64)
+            scales = mx.tile([P, columns], U8, name=name + "_scales", align_bytes=64)
             nc.vector.quantize_mx(out=codes[:].bitcast(FP8X4), scales=scales[:], in_=grouped)
             return codes, scales
 
-        def mx_pass(acc, weight, i, rows, start, stop):
+        def mx_pass(acc, m, weight, i, rows, start, stop):
             units = slice(i * P, (i + 1) * P)
             nc.tensor.matmul_mx(
-                out=acc[:],
+                out=acc[:, m * CHUNK : (m + 1) * CHUNK],
                 lhsT=weight[0][:, units].bitcast(FP8X4),
                 lhsT_scale=weight[1][:, units],
                 rhs=rows[0][:].bitcast(FP8X4),
@@ -124,90 +130,133 @@ def tile_augru_pa_kernel(
 
         x_mx = [None] * N_CHUNKS
         h_mx = [None] * N_CHUNKS
-        x_grouped = transpose_rows("x_grouped0", x_raw[0])
-        h_grouped = transpose_rows("h_grouped0", h_raw[0])
-        x_mx[0] = quantise("x0", x_grouped)
+        gate = [[None] * PAIRS for c in range(N_CHUNKS)]
+        state_bank = [[None] * PAIRS for c in range(N_CHUNKS)]
+        gated = [[None] * PAIRS for c in range(N_CHUNKS)]
+        summed = [[None] * PAIRS for c in range(N_CHUNKS)]
+
+        def reset_gate(c):
+            for j in range(PAIRS):
+                acc = banks.tile([P, BANK], F32, tag="bank")
+                for m in range(PAIR):
+                    mx_pass(acc, m, wxr, j * PAIR + m, x_mx[c], True, False)
+                    mx_pass(acc, m, whr, j * PAIR + m, h_mx[c], False, True)
+                r = work.tile([P, BANK], F32, tag="gate")
+                for m in range(PAIR):
+                    i = j * PAIR + m
+                    nc.scalar.activation(
+                        out=r[:, m * CHUNK : (m + 1) * CHUNK],
+                        in_=acc[:, m * CHUNK : (m + 1) * CHUNK],
+                        func=ACT.Sigmoid,
+                        bias=bias[:, i : i + 1],
+                    )
+                gate[c][j] = r
+
+        def state_product(c):
+            for j in range(PAIRS):
+                acc = banks.tile([P, BANK], F32, tag="bank")
+                for m in range(PAIR):
+                    mx_pass(acc, m, whh, j * PAIR + m, h_mx[c], True, True)
+                state_bank[c][j] = acc
+
+        def gated_state(c):
+            for j in range(PAIRS):
+                product = work.tile([P, BANK], F32, tag="gated")
+                nc.vector.tensor_tensor(
+                    out=product[:], in0=gate[c][j][:], in1=state_bank[c][j][:], op=ALU.mult
+                )
+                gated[c][j] = product
+
+        def candidate_sum(c):
+            for j in range(PAIRS):
+                acc = banks.tile([P, BANK], F32, tag="bank")
+                for m in range(PAIR):
+                    mx_pass(acc, m, wxh, j * PAIR + m, x_mx[c], True, True)
+                total = work.tile([P, BANK], F32, tag="summed")
+                for m in range(PAIR):
+                    i = UNIT_TILES + j * PAIR + m
+                    nc.vector.scalar_tensor_tensor(
+                        out=total[:, m * CHUNK : (m + 1) * CHUNK],
+                        in0=acc[:, m * CHUNK : (m + 1) * CHUNK],
+                        scalar=bias[:, i : i + 1],
+                        in1=gated[c][j][:, m * CHUNK : (m + 1) * CHUNK],
+                        op0=ALU.add,
+                        op1=ALU.add,
+                    )
+                summed[c][j] = total
+
+        def finish(c):
+            for j in range(PAIRS):
+                bank = banks.tile([P, BANK], F32, tag="bank")
+                for m in range(PAIR):
+                    for t in range(ROW_TILES):
+                        nc.tensor.transpose(
+                            out=bank[:, (t * PAIR + m) * P : (t * PAIR + m + 1) * P],
+                            in_=summed[c][j][:, m * CHUNK + t * P : m * CHUNK + (t + 1) * P],
+                            identity=ident[:],
+                        )
+                result = work.tile([P, BANK], F32, tag="result")
+                nc.scalar.activation(out=result[:], in_=bank[:], func=ACT.Tanh)
+                nc.sync.dma_start(
+                    out=out[
+                        c * CHUNK : (c + 1) * CHUNK, j * PAIR * P : (j + 1) * PAIR * P
+                    ].rearrange("(p t) n -> p t n", t=ROW_TILES),
+                    in_=result[:].rearrange("p (t n) -> p t n", t=ROW_TILES),
+                )
+
         wxr_grouped = regroup_weight("wxr_grouped", wxr_raw)
-        h_mx[0] = quantise("h0", h_grouped)
-        whr_grouped = regroup_weight("whr_grouped", whr_raw)
-        wxr = quantise("wxr", wxr_grouped)
-        whr = quantise("whr", whr_grouped)
-        x_grouped = transpose_rows("x_grouped1", x_raw[1])
-        whh_grouped = regroup_weight("whh_grouped", whh_raw)
-        x_mx[1] = quantise("x1", x_grouped)
-        whh = quantise("whh", whh_grouped)
-        h_grouped = transpose_rows("h_grouped1", h_raw[1])
-        wxh_grouped = regroup_weight("wxh_grouped", wxh_raw)
-        bias_bank = banks.tile([P, CHUNK], F32, tag="bank")
+        x_bank = transpose_rows(x_raw[0])
+        x_grouped = group_rows("x_grouped0", x_bank)
+        wxr = quantise("wxr", wxr_grouped, UNITS)
+        h_bank = transpose_rows(h_raw[0])
+        h_grouped = group_rows("h_grouped0", h_bank)
+        bias_bank = banks.tile([P, BANK], F32, tag="bank")
         nc.tensor.transpose(out=bias_bank[:, 0:P], in_=bias_square[:], identity=ident[:])
+        x_mx[0] = quantise("x0", x_grouped, CHUNK)
+        whr_grouped = regroup_weight("whr_grouped", whr_raw)
+        h_mx[0] = quantise("h0", h_grouped, CHUNK)
         bias = const.tile([P, 2 * UNIT_TILES], F32)
         nc.vector.tensor_copy(out=bias[:], in_=bias_bank[:, 0 : 2 * UNIT_TILES])
-        h_mx[1] = quantise("h1", h_grouped)
-        wxh = quantise("wxh", wxh_grouped)
-
-        gate = [[None] * UNIT_TILES for c in range(N_CHUNKS)]
-        gated = [[None] * UNIT_TILES for c in range(N_CHUNKS)]
-        summed = [[None] * UNIT_TILES for c in range(N_CHUNKS)]
-
-        def reset_gate(c, i):
-            acc = banks.tile([P, CHUNK], F32, tag="bank")
-            mx_pass(acc, wxr, i, x_mx[c], True, False)
-            mx_pass(acc, whr, i, h_mx[c], False, True)
-            r = work.tile([P, CHUNK], F32, tag="gate")
-            nc.scalar.activation(out=r[:], in_=acc[:], func=ACT.Sigmoid, bias=bias[:, i : i + 1])
-            gate[c][i] = r
-
-        def gated_state(c, i):
-            acc = banks.tile([P, CHUNK], F32, tag="bank")
-            mx_pass(acc, whh, i, h_mx[c], True, True)
-            product = work.tile([P, CHUNK], F32, tag="gated")
-            nc.vector.tensor_tensor(out=product[:], in0=gate[c][i][:], in1=acc[:], op=ALU.mult)
-            gated[c][i] = product
-
-        def candidate_sum(c, i):
-            acc = banks.tile([P, CHUNK], F32, tag="bank")
-            mx_pass(acc, wxh, i, x_mx[c], True, True)
-            total = work.tile([P, CHUNK], F32, tag="summed")
-            nc.vector.scalar_tensor_tensor(
-                out=total[:],
-                in0=acc[:],
-                scalar=bias[:, UNIT_TILES + i : UNIT_TILES + i + 1],
-                in1=gated[c][i][:],
-                op0=ALU.add,
-                op1=ALU.add,
-            )
-            summed[c][i] = total
-
-        def finish(c, i):
-            bank = banks.tile([P, CHUNK], F32, tag="bank")
-            for t in range(ROW_TILES):
-                nc.tensor.transpose(
-                    out=bank[:, t * P : (t + 1) * P],
-                    in_=summed[c][i][:, t * P : (t + 1) * P],
-                    identity=ident[:],
-                )
-            result = work.tile([P, CHUNK], F32, tag="result")
-            nc.scalar.activation(out=result[:], in_=bank[:], func=ACT.Tanh)
-            nc.sync.dma_start(
-                out=out[c * CHUNK : (c + 1) * CHUNK, i * P : (i + 1) * P].rearrange(
-                    "(p t) n -> p t n", t=ROW_TILES
-                ),
-                in_=result[:].rearrange("p (t n) -> p t n", t=ROW_TILES),
-            )
-
-        for i in range(UNIT_TILES):
-            reset_gate(0, i)
-        for i in range(UNIT_TILES):
-            gated_state(0, i)
-        for i in range(UNIT_TILES):
-            candidate_sum(0, i)
-        for i in range(UNIT_TILES):
-            reset_gate(1, i)
-        for i in range(UNIT_TILES):
-            gated_state(1, i)
-        for i in range(UNIT_TILES):
-            finish(0, i)
-        for i in range(UNIT_TILES):
-            candidate_sum(1, i)
-        for i in range(UNIT_TILES):
-            finish(1, i)
+        whr = quantise("whr", whr_grouped, UNITS)
+        x_bank = transpose_rows(x_raw[1])
+        whh_grouped = regroup_weight("whh_grouped", whh_raw)
+        x_grouped = group_rows("x_grouped1", x_bank)
+        reset_gate(0)
+        x_mx[1] = quantise("x1", x_grouped, CHUNK)
+        whh = quantise("whh", whh_grouped, UNITS)
+        h_bank = transpose_rows(h_raw[1])
+        h_grouped = group_rows("h_grouped1", h_bank)
+        state_product(0)
+        wxh_grouped = regroup_weight("wxh_grouped", wxh_raw)
+        h_mx[1] = quantise("h1", h_grouped, CHUNK)
+        gated_state(0)
+        x_bank = transpose_rows(x_raw[2])
+        x_grouped = group_rows("x_grouped2", x_bank)
+        reset_gate(1)
+        h_bank = transpose_rows(h_raw[2])
+        h_grouped = group_rows("h_grouped2", h_bank)
+        wxh = quantise("wxh", wxh_grouped, UNITS)
+        x_mx[2] = quantise("x2", x_grouped, CHUNK)
+        candidate_sum(0)
+        state_product(1)
+        h_mx[2] = quantise("h2", h_grouped, CHUNK)
+        gated_state(1)
+        x_bank = transpose_rows(x_raw[3])
+        x_grouped = group_rows("x_grouped3", x_bank)
+        h_bank = transpose_rows(h_raw[3])
+        finish(0)
+        h_grouped = group_rows("h_grouped3", h_bank)
+        x_mx[3] = quantise("x3", x_grouped, CHUNK)
+        candidate_sum(1)
+        h_mx[3] = quantise("h3", h_grouped, CHUNK)
+        reset_gate(2)
+        state_product(2)
+        gated_state(2)
+        finish(1)
+        candidate_sum(2)
+        reset_gate(3)
+        state_product(3)
+        gated_state(3)
+        finish(2)
+        candidate_sum(3)
+        finish(3)

@@ -28,6 +28,9 @@ RUN = 4
 COLUMN_RUNS = UNITS // RUN
 VECTOR_RUNS = 5 * COLUMN_RUNS // 8
 
+IDLE_HEAD = 4
+IDLE_LOADS = 2
+
 FLOPS = 4 * 2 * BATCH * K * UNITS
 
 
@@ -50,6 +53,19 @@ def tile_augru_pa_kernel(
         nc.scalar.activation(out=warm[:, 1:2], in_=warm[:, 0:1], func=ACT.Sigmoid)
         ident = const.tile([P, P], F32)
         make_identity(nc, ident[:])
+        idle_zeros = const.tile([P, P + BANK], BF16)
+        nc.vector.memset(idle_zeros[:], 0.0)
+        idle_bank = banks.tile([P, BANK], F32, tag="bank")
+
+        def keep_clock(count):
+            for n in range(count):
+                nc.tensor.matmul(
+                    out=idle_bank[:],
+                    lhsT=idle_zeros[:, 0:P],
+                    rhs=idle_zeros[:, P : P + BANK],
+                    start=True,
+                    stop=True,
+                )
 
         def load_rows(name, tensor, c):
             tile = raw.tile([P, ROW_TILES * K], BF16, name=name)
@@ -64,21 +80,22 @@ def tile_augru_pa_kernel(
 
         x_raw = [None] * N_CHUNKS
         h_raw = [None] * N_CHUNKS
-        wxr_raw = load_weight("wxr_raw", Wx_r)
         x_raw[0] = load_rows("x_raw0", input_x, 0)
+        wxr_raw = load_weight("wxr_raw", Wx_r)
         h_raw[0] = load_rows("h_raw0", input_h, 0)
         nc.sync.dma_start(out=bias_rows[0:UNIT_TILES, :], in_=b_r.rearrange("(i n) -> i n", n=P))
         nc.sync.dma_start(
             out=bias_rows[UNIT_TILES : 2 * UNIT_TILES, :], in_=b_h.rearrange("(i n) -> i n", n=P)
         )
         whr_raw = load_weight("whr_raw", Wh_r)
-        whh_raw = load_weight("whh_raw", Wh_h)
         x_raw[1] = load_rows("x_raw1", input_x, 1)
+        whh_raw = load_weight("whh_raw", Wh_h)
         h_raw[1] = load_rows("h_raw1", input_h, 1)
+        x_raw[2] = load_rows("x_raw2", input_x, 2)
         wxh_raw = load_weight("wxh_raw", Wx_h)
-        for c in range(2, N_CHUNKS):
-            x_raw[c] = load_rows("x_raw%d" % c, input_x, c)
-            h_raw[c] = load_rows("h_raw%d" % c, input_h, c)
+        h_raw[2] = load_rows("h_raw2", input_h, 2)
+        x_raw[3] = load_rows("x_raw3", input_x, 3)
+        h_raw[3] = load_rows("h_raw3", input_h, 3)
         bias_square = const.tile([P, P], F32)
         nc.gpsimd.tensor_copy(out=bias_square[:], in_=bias_rows[:])
 
@@ -196,14 +213,24 @@ def tile_augru_pa_kernel(
                             identity=ident[:],
                         )
                 result = work.tile([P, BANK], F32, tag="result")
-                nc.scalar.activation(out=result[:], in_=bank[:], func=ACT.Tanh)
-                nc.sync.dma_start(
-                    out=out[
-                        c * CHUNK : (c + 1) * CHUNK, j * PAIR * P : (j + 1) * PAIR * P
-                    ].rearrange("(p t) n -> p t n", t=ROW_TILES),
-                    in_=result[:].rearrange("p (t n) -> p t n", t=ROW_TILES),
-                )
+                turned = bank[:].rearrange("p (t n) -> p t n", t=ROW_TILES)
+                stored = result[:].rearrange("p (t n) -> p t n", t=ROW_TILES)
+                parts = PAIR if c == N_CHUNKS - 1 and j == PAIRS - 1 else 1
+                width = PAIR * P // parts
+                for part in range(parts):
+                    cols = slice(part * width, (part + 1) * width)
+                    first = j * PAIR * P + part * width
+                    nc.scalar.activation(
+                        out=stored[:, :, cols], in_=turned[:, :, cols], func=ACT.Tanh
+                    )
+                    nc.sync.dma_start(
+                        out=out[c * CHUNK : (c + 1) * CHUNK, first : first + width].rearrange(
+                            "(p t) n -> p t n", t=ROW_TILES
+                        ),
+                        in_=stored[:, :, cols],
+                    )
 
+        keep_clock(IDLE_HEAD)
         wxr_grouped = regroup_weight("wxr_grouped", wxr_raw)
         x_bank = transpose_rows(x_raw[0])
         x_grouped = group_rows("x_grouped0", x_bank)
@@ -212,6 +239,7 @@ def tile_augru_pa_kernel(
         h_grouped = group_rows("h_grouped0", h_bank)
         bias_bank = banks.tile([P, BANK], F32, tag="bank")
         nc.tensor.transpose(out=bias_bank[:, 0:P], in_=bias_square[:], identity=ident[:])
+        keep_clock(IDLE_LOADS)
         x_mx[0] = quantise("x0", x_grouped, CHUNK)
         whr_grouped = regroup_weight("whr_grouped", whr_raw)
         h_mx[0] = quantise("h0", h_grouped, CHUNK)
@@ -219,33 +247,33 @@ def tile_augru_pa_kernel(
         nc.vector.tensor_copy(out=bias[:], in_=bias_bank[:, 0 : 2 * UNIT_TILES])
         whr = quantise("whr", whr_grouped, UNITS)
         x_bank = transpose_rows(x_raw[1])
-        whh_grouped = regroup_weight("whh_grouped", whh_raw)
         x_grouped = group_rows("x_grouped1", x_bank)
+        whh_grouped = regroup_weight("whh_grouped", whh_raw)
         reset_gate(0)
         x_mx[1] = quantise("x1", x_grouped, CHUNK)
         whh = quantise("whh", whh_grouped, UNITS)
         h_bank = transpose_rows(h_raw[1])
         h_grouped = group_rows("h_grouped1", h_bank)
-        state_product(0)
         wxh_grouped = regroup_weight("wxh_grouped", wxh_raw)
-        h_mx[1] = quantise("h1", h_grouped, CHUNK)
-        gated_state(0)
         x_bank = transpose_rows(x_raw[2])
         x_grouped = group_rows("x_grouped2", x_bank)
+        state_product(0)
+        h_mx[1] = quantise("h1", h_grouped, CHUNK)
+        gated_state(0)
         reset_gate(1)
         h_bank = transpose_rows(h_raw[2])
         h_grouped = group_rows("h_grouped2", h_bank)
+        x_bank = transpose_rows(x_raw[3])
         wxh = quantise("wxh", wxh_grouped, UNITS)
         x_mx[2] = quantise("x2", x_grouped, CHUNK)
+        x_grouped = group_rows("x_grouped3", x_bank)
         candidate_sum(0)
         state_product(1)
         h_mx[2] = quantise("h2", h_grouped, CHUNK)
         gated_state(1)
-        x_bank = transpose_rows(x_raw[3])
-        x_grouped = group_rows("x_grouped3", x_bank)
         h_bank = transpose_rows(h_raw[3])
-        finish(0)
         h_grouped = group_rows("h_grouped3", h_bank)
+        finish(0)
         x_mx[3] = quantise("x3", x_grouped, CHUNK)
         candidate_sum(1)
         h_mx[3] = quantise("h3", h_grouped, CHUNK)
@@ -257,6 +285,6 @@ def tile_augru_pa_kernel(
         reset_gate(3)
         state_product(3)
         gated_state(3)
-        finish(2)
         candidate_sum(3)
+        finish(2)
         finish(3)

@@ -25,8 +25,7 @@ PAIRS = UNIT_TILES // PAIR
 BANK = PAIR * CHUNK
 WORDS = K // 2
 RUN = 4
-COLUMN_RUNS = UNITS // RUN
-VECTOR_RUNS = 5 * COLUMN_RUNS // 8
+VECTOR_SHARE = (5, 8)
 
 IDLE_HEAD = 4
 IDLE_LOADS = 2
@@ -53,7 +52,7 @@ def tile_augru_pa_kernel(
         nc.scalar.activation(out=warm[:, 1:2], in_=warm[:, 0:1], func=ACT.Sigmoid)
         ident = const.tile([P, P], F32)
         make_identity(nc, ident[:])
-        idle_zeros = const.tile([P, P + BANK], BF16)
+        idle_zeros = const.tile([P, BANK], BF16)
         nc.vector.memset(idle_zeros[:], 0.0)
         idle_bank = banks.tile([P, BANK], F32, tag="bank")
 
@@ -62,7 +61,7 @@ def tile_augru_pa_kernel(
                 nc.tensor.matmul(
                     out=idle_bank[:],
                     lhsT=idle_zeros[:, 0:P],
-                    rhs=idle_zeros[:, P : P + BANK],
+                    rhs=idle_zeros[:],
                     start=True,
                     stop=True,
                 )
@@ -80,8 +79,8 @@ def tile_augru_pa_kernel(
 
         x_raw = [None] * N_CHUNKS
         h_raw = [None] * N_CHUNKS
-        x_raw[0] = load_rows("x_raw0", input_x, 0)
         wxr_raw = load_weight("wxr_raw", Wx_r)
+        x_raw[0] = load_rows("x_raw0", input_x, 0)
         h_raw[0] = load_rows("h_raw0", input_h, 0)
         nc.sync.dma_start(out=bias_rows[0:UNIT_TILES, :], in_=b_r.rearrange("(i n) -> i n", n=P))
         nc.sync.dma_start(
@@ -119,12 +118,15 @@ def tile_augru_pa_kernel(
             )
             return grouped[:]
 
-        def regroup_weight(name, weight_raw):
-            grouped = mx.tile([P, UNITS, PACK], BF16, name=name, align_bytes=64)
+        def regroup_weight(name, weight_raw, first=0, pairs=PAIRS):
+            units = pairs * PAIR * P
+            grouped = mx.tile([P, units, PACK], BF16, name=name, align_bytes=64)
+            raw_units = weight_raw[:, :, first * PAIR * P : first * PAIR * P + units]
             dst = grouped[:].rearrange("q (c i) t -> q c t i", i=RUN)
-            src = weight_raw[:].rearrange("q t (c i) -> q c t i", i=RUN)
-            nc.vector.tensor_copy(out=dst[:, :VECTOR_RUNS], in_=src[:, :VECTOR_RUNS])
-            nc.scalar.copy(out=dst[:, VECTOR_RUNS:], in_=src[:, VECTOR_RUNS:])
+            src = raw_units.rearrange("q t (c i) -> q c t i", i=RUN)
+            cut = units // RUN * VECTOR_SHARE[0] // VECTOR_SHARE[1]
+            nc.vector.tensor_copy(out=dst[:, :cut], in_=src[:, :cut])
+            nc.scalar.copy(out=dst[:, cut:], in_=src[:, cut:])
             return grouped[:].rearrange("q n t -> q (n t)")
 
         def quantise(name, grouped, columns):
@@ -133,8 +135,16 @@ def tile_augru_pa_kernel(
             nc.vector.quantize_mx(out=codes[:].bitcast(FP8X4), scales=scales[:], in_=grouped)
             return codes, scales
 
-        def mx_pass(acc, m, weight, i, rows, start, stop):
-            units = slice(i * P, (i + 1) * P)
+        def quantise_weight(name, grouped, pairs=PAIRS):
+            codes, scales = quantise(name, grouped, pairs * PAIR * P)
+            width = PAIR * P
+            return [
+                (codes[:, j * width : (j + 1) * width], scales[:, j * width : (j + 1) * width])
+                for j in range(pairs)
+            ]
+
+        def mx_pass(acc, m, weight, rows, start, stop):
+            units = slice(m * P, (m + 1) * P)
             nc.tensor.matmul_mx(
                 out=acc[:, m * CHUNK : (m + 1) * CHUNK],
                 lhsT=weight[0][:, units].bitcast(FP8X4),
@@ -156,8 +166,8 @@ def tile_augru_pa_kernel(
             for j in range(PAIRS):
                 acc = banks.tile([P, BANK], F32, tag="bank")
                 for m in range(PAIR):
-                    mx_pass(acc, m, wxr, j * PAIR + m, x_mx[c], True, False)
-                    mx_pass(acc, m, whr, j * PAIR + m, h_mx[c], False, True)
+                    mx_pass(acc, m, wxr[j], x_mx[c], True, False)
+                    mx_pass(acc, m, whr[j], h_mx[c], False, True)
                 r = work.tile([P, BANK], F32, tag="gate")
                 for m in range(PAIR):
                     i = j * PAIR + m
@@ -173,7 +183,7 @@ def tile_augru_pa_kernel(
             for j in range(PAIRS):
                 acc = banks.tile([P, BANK], F32, tag="bank")
                 for m in range(PAIR):
-                    mx_pass(acc, m, whh, j * PAIR + m, h_mx[c], True, True)
+                    mx_pass(acc, m, whh[j], h_mx[c], True, True)
                 state_bank[c][j] = acc
 
         def gated_state(c):
@@ -188,7 +198,7 @@ def tile_augru_pa_kernel(
             for j in range(PAIRS):
                 acc = banks.tile([P, BANK], F32, tag="bank")
                 for m in range(PAIR):
-                    mx_pass(acc, m, wxh, j * PAIR + m, x_mx[c], True, True)
+                    mx_pass(acc, m, wxh[j], x_mx[c], True, True)
                 total = work.tile([P, BANK], F32, tag="summed")
                 for m in range(PAIR):
                     i = UNIT_TILES + j * PAIR + m
@@ -234,24 +244,26 @@ def tile_augru_pa_kernel(
         wxr_grouped = regroup_weight("wxr_grouped", wxr_raw)
         x_bank = transpose_rows(x_raw[0])
         x_grouped = group_rows("x_grouped0", x_bank)
-        wxr = quantise("wxr", wxr_grouped, UNITS)
+        wxr = quantise_weight("wxr", wxr_grouped)
         h_bank = transpose_rows(h_raw[0])
         h_grouped = group_rows("h_grouped0", h_bank)
         bias_bank = banks.tile([P, BANK], F32, tag="bank")
         nc.tensor.transpose(out=bias_bank[:, 0:P], in_=bias_square[:], identity=ident[:])
         keep_clock(IDLE_LOADS)
         x_mx[0] = quantise("x0", x_grouped, CHUNK)
-        whr_grouped = regroup_weight("whr_grouped", whr_raw)
+        whr_grouped = [regroup_weight("whr_grouped%d" % j, whr_raw, j, 1) for j in range(PAIRS)]
         h_mx[0] = quantise("h0", h_grouped, CHUNK)
+        whr = quantise_weight("whr0", whr_grouped[0], 1)
         bias = const.tile([P, 2 * UNIT_TILES], F32)
         nc.vector.tensor_copy(out=bias[:], in_=bias_bank[:, 0 : 2 * UNIT_TILES])
-        whr = quantise("whr", whr_grouped, UNITS)
+        whr = whr + quantise_weight("whr1", whr_grouped[1], 1)
         x_bank = transpose_rows(x_raw[1])
         x_grouped = group_rows("x_grouped1", x_bank)
-        whh_grouped = regroup_weight("whh_grouped", whh_raw)
+        whh_grouped = [regroup_weight("whh_grouped%d" % j, whh_raw, j, 1) for j in range(PAIRS)]
         reset_gate(0)
         x_mx[1] = quantise("x1", x_grouped, CHUNK)
-        whh = quantise("whh", whh_grouped, UNITS)
+        whh = quantise_weight("whh0", whh_grouped[0], 1)
+        whh = whh + quantise_weight("whh1", whh_grouped[1], 1)
         h_bank = transpose_rows(h_raw[1])
         h_grouped = group_rows("h_grouped1", h_bank)
         wxh_grouped = regroup_weight("wxh_grouped", wxh_raw)
@@ -260,11 +272,11 @@ def tile_augru_pa_kernel(
         state_product(0)
         h_mx[1] = quantise("h1", h_grouped, CHUNK)
         gated_state(0)
-        reset_gate(1)
         h_bank = transpose_rows(h_raw[2])
+        reset_gate(1)
         h_grouped = group_rows("h_grouped2", h_bank)
         x_bank = transpose_rows(x_raw[3])
-        wxh = quantise("wxh", wxh_grouped, UNITS)
+        wxh = quantise_weight("wxh", wxh_grouped)
         x_mx[2] = quantise("x2", x_grouped, CHUNK)
         x_grouped = group_rows("x_grouped3", x_bank)
         candidate_sum(0)

@@ -130,8 +130,8 @@ def tile_augru_pa_kernel(
             return grouped[:].rearrange("q n t -> q (n t)")
 
         def quantise(name, grouped, columns):
-            codes = mx.tile([P, columns], U32, name=name + "_codes", align_bytes=64)
-            scales = mx.tile([P, columns], U8, name=name + "_scales", align_bytes=64)
+            codes = mx.tile([P, columns], U32, name=name + "_codes", align_bytes=256)
+            scales = mx.tile([P, columns], U8, name=name + "_scales", align_bytes=256)
             nc.vector.quantize_mx(out=codes[:].bitcast(FP8X4), scales=scales[:], in_=grouped)
             return codes, scales
 

@@ -24,7 +24,7 @@ PAIR = 2
 PAIRS = UNIT_TILES // PAIR
 BANK = PAIR * CHUNK
 WORDS = K // 2
-RUN = 4
+RUN = 8
 VECTOR_SHARE = (5, 8)
 
 IDLE_HEAD = 4

@@ -160,85 +160,87 @@ def tile_augru_pa_kernel(
         gate = [[None] * PAIRS for c in range(N_CHUNKS)]
         state_bank = [[None] * PAIRS for c in range(N_CHUNKS)]
         gated = [[None] * PAIRS for c in range(N_CHUNKS)]
+        candidate_bank = [[None] * PAIRS for c in range(N_CHUNKS)]
         summed = [[None] * PAIRS for c in range(N_CHUNKS)]
 
-        def reset_gate(c):
-            for j in range(PAIRS):
-                acc = banks.tile([P, BANK], F32, tag="bank")
-                for m in range(PAIR):
-                    mx_pass(acc, m, wxr[j], x_mx[c], True, False)
-                    mx_pass(acc, m, whr[j], h_mx[c], False, True)
-                r = work.tile([P, BANK], F32, tag="gate")
-                for m in range(PAIR):
-                    i = j * PAIR + m
-                    nc.scalar.activation(
-                        out=r[:, m * CHUNK : (m + 1) * CHUNK],
-                        in_=acc[:, m * CHUNK : (m + 1) * CHUNK],
-                        func=ACT.Sigmoid,
-                        bias=bias[:, i : i + 1],
-                    )
-                gate[c][j] = r
-
-        def state_product(c):
-            for j in range(PAIRS):
-                acc = banks.tile([P, BANK], F32, tag="bank")
-                for m in range(PAIR):
-                    mx_pass(acc, m, whh[j], h_mx[c], True, True)
-                state_bank[c][j] = acc
-
-        def gated_state(c):
-            for j in range(PAIRS):
-                product = work.tile([P, BANK], F32, tag="gated")
-                nc.vector.tensor_tensor(
-                    out=product[:], in0=gate[c][j][:], in1=state_bank[c][j][:], op=ALU.mult
+        def reset_gate(c, j):
+            acc = banks.tile([P, BANK], F32, tag="bank")
+            for m in range(PAIR):
+                mx_pass(acc, m, wxr[j], x_mx[c], True, False)
+                mx_pass(acc, m, whr[j], h_mx[c], False, True)
+            r = work.tile([P, BANK], F32, tag="gate")
+            for m in range(PAIR):
+                i = j * PAIR + m
+                nc.scalar.activation(
+                    out=r[:, m * CHUNK : (m + 1) * CHUNK],
+                    in_=acc[:, m * CHUNK : (m + 1) * CHUNK],
+                    func=ACT.Sigmoid,
+                    bias=bias[:, i : i + 1],
                 )
-                gated[c][j] = product
+            gate[c][j] = r
 
-        def candidate_sum(c):
-            for j in range(PAIRS):
-                acc = banks.tile([P, BANK], F32, tag="bank")
-                for m in range(PAIR):
-                    mx_pass(acc, m, wxh[j], x_mx[c], True, True)
-                total = work.tile([P, BANK], F32, tag="summed")
-                for m in range(PAIR):
-                    i = UNIT_TILES + j * PAIR + m
-                    nc.vector.scalar_tensor_tensor(
-                        out=total[:, m * CHUNK : (m + 1) * CHUNK],
-                        in0=acc[:, m * CHUNK : (m + 1) * CHUNK],
-                        scalar=bias[:, i : i + 1],
-                        in1=gated[c][j][:, m * CHUNK : (m + 1) * CHUNK],
-                        op0=ALU.add,
-                        op1=ALU.add,
-                    )
-                summed[c][j] = total
+        def state_product(c, j):
+            acc = banks.tile([P, BANK], F32, tag="bank")
+            for m in range(PAIR):
+                mx_pass(acc, m, whh[j], h_mx[c], True, True)
+            state_bank[c][j] = acc
 
-        def finish(c):
+        def gated_state(c, j):
+            product = work.tile([P, BANK], F32, tag="gated")
+            nc.vector.tensor_tensor(
+                out=product[:], in0=gate[c][j][:], in1=state_bank[c][j][:], op=ALU.mult
+            )
+            gated[c][j] = product
+
+        def candidate_product(c, j):
+            acc = banks.tile([P, BANK], F32, tag="bank")
+            for m in range(PAIR):
+                mx_pass(acc, m, wxh[j], x_mx[c], True, True)
+            candidate_bank[c][j] = acc
+
+        def candidate_sum(c, j):
+            acc = candidate_bank[c][j]
+            total = work.tile([P, BANK], F32, tag="summed")
+            for m in range(PAIR):
+                i = UNIT_TILES + j * PAIR + m
+                nc.vector.scalar_tensor_tensor(
+                    out=total[:, m * CHUNK : (m + 1) * CHUNK],
+                    in0=acc[:, m * CHUNK : (m + 1) * CHUNK],
+                    scalar=bias[:, i : i + 1],
+                    in1=gated[c][j][:, m * CHUNK : (m + 1) * CHUNK],
+                    op0=ALU.add,
+                    op1=ALU.add,
+                )
+            summed[c][j] = total
+
+        def finish(c, j):
+            bank = banks.tile([P, BANK], F32, tag="bank")
+            for m in range(PAIR):
+                for t in range(ROW_TILES):
+                    nc.tensor.transpose(
+                        out=bank[:, (t * PAIR + m) * P : (t * PAIR + m + 1) * P],
+                        in_=summed[c][j][:, m * CHUNK + t * P : m * CHUNK + (t + 1) * P],
+                        identity=ident[:],
+                    )
+            result = work.tile([P, BANK], F32, tag="result")
+            turned = bank[:].rearrange("p (t n) -> p t n", t=ROW_TILES)
+            stored = result[:].rearrange("p (t n) -> p t n", t=ROW_TILES)
+            parts = PAIR if c == N_CHUNKS - 1 and j == PAIRS - 1 else 1
+            width = PAIR * P // parts
+            for part in range(parts):
+                cols = slice(part * width, (part + 1) * width)
+                first = j * PAIR * P + part * width
+                nc.scalar.activation(out=stored[:, :, cols], in_=turned[:, :, cols], func=ACT.Tanh)
+                nc.sync.dma_start(
+                    out=out[c * CHUNK : (c + 1) * CHUNK, first : first + width].rearrange(
+                        "(p t) n -> p t n", t=ROW_TILES
+                    ),
+                    in_=stored[:, :, cols],
+                )
+
+        def both(step, c):
             for j in range(PAIRS):
-                bank = banks.tile([P, BANK], F32, tag="bank")
-                for m in range(PAIR):
-                    for t in range(ROW_TILES):
-                        nc.tensor.transpose(
-                            out=bank[:, (t * PAIR + m) * P : (t * PAIR + m + 1) * P],
-                            in_=summed[c][j][:, m * CHUNK + t * P : m * CHUNK + (t + 1) * P],
-                            identity=ident[:],
-                        )
-                result = work.tile([P, BANK], F32, tag="result")
-                turned = bank[:].rearrange("p (t n) -> p t n", t=ROW_TILES)
-                stored = result[:].rearrange("p (t n) -> p t n", t=ROW_TILES)
-                parts = PAIR if c == N_CHUNKS - 1 and j == PAIRS - 1 else 1
-                width = PAIR * P // parts
-                for part in range(parts):
-                    cols = slice(part * width, (part + 1) * width)
-                    first = j * PAIR * P + part * width
-                    nc.scalar.activation(
-                        out=stored[:, :, cols], in_=turned[:, :, cols], func=ACT.Tanh
-                    )
-                    nc.sync.dma_start(
-                        out=out[c * CHUNK : (c + 1) * CHUNK, first : first + width].rearrange(
-                            "(p t) n -> p t n", t=ROW_TILES
-                        ),
-                        in_=stored[:, :, cols],
-                    )
+                step(c, j)
 
         keep_clock(IDLE_HEAD)
         wxr_grouped = regroup_weight("wxr_grouped", wxr_raw)
@@ -260,7 +262,7 @@ def tile_augru_pa_kernel(
         x_bank = transpose_rows(x_raw[1])
         x_grouped = group_rows("x_grouped1", x_bank)
         whh_grouped = [regroup_weight("whh_grouped%d" % j, whh_raw, j, 1) for j in range(PAIRS)]
-        reset_gate(0)
+        both(reset_gate, 0)
         x_mx[1] = quantise("x1", x_grouped, CHUNK)
         whh = quantise_weight("whh0", whh_grouped[0], 1)
         whh = whh + quantise_weight("whh1", whh_grouped[1], 1)
@@ -269,34 +271,45 @@ def tile_augru_pa_kernel(
         wxh_grouped = regroup_weight("wxh_grouped", wxh_raw)
         x_bank = transpose_rows(x_raw[2])
         x_grouped = group_rows("x_grouped2", x_bank)
-        state_product(0)
+        both(state_product, 0)
         h_mx[1] = quantise("h1", h_grouped, CHUNK)
-        gated_state(0)
-        h_bank = transpose_rows(h_raw[2])
-        reset_gate(1)
-        h_grouped = group_rows("h_grouped2", h_bank)
-        x_bank = transpose_rows(x_raw[3])
+        gated_state(0, 0)
         wxh = quantise_weight("wxh", wxh_grouped)
+        gated_state(0, 1)
+        h_bank = transpose_rows(h_raw[2])
+        both(reset_gate, 1)
+        h_grouped = group_rows("h_grouped2", h_bank)
         x_mx[2] = quantise("x2", x_grouped, CHUNK)
-        x_grouped = group_rows("x_grouped3", x_bank)
-        candidate_sum(0)
-        state_product(1)
+        both(candidate_product, 0)
+        both(candidate_sum, 0)
+        both(state_product, 1)
         h_mx[2] = quantise("h2", h_grouped, CHUNK)
-        gated_state(1)
+        both(gated_state, 1)
+        x_bank = transpose_rows(x_raw[3])
+        x_grouped = group_rows("x_grouped3", x_bank)
         h_bank = transpose_rows(h_raw[3])
         h_grouped = group_rows("h_grouped3", h_bank)
-        finish(0)
+        both(finish, 0)
         x_mx[3] = quantise("x3", x_grouped, CHUNK)
-        candidate_sum(1)
+        both(candidate_product, 1)
+        both(candidate_sum, 1)
         h_mx[3] = quantise("h3", h_grouped, CHUNK)
-        reset_gate(2)
-        state_product(2)
-        gated_state(2)
-        finish(1)
-        candidate_sum(2)
-        reset_gate(3)
-        state_product(3)
-        gated_state(3)
-        candidate_sum(3)
-        finish(2)
-        finish(3)
+        both(reset_gate, 2)
+        both(state_product, 2)
+        both(gated_state, 2)
+        both(finish, 1)
+        candidate_product(2, 0)
+        reset_gate(3, 0)
+        candidate_product(2, 1)
+        both(candidate_sum, 2)
+        state_product(3, 0)
+        gated_state(3, 0)
+        reset_gate(3, 1)
+        state_product(3, 1)
+        candidate_product(3, 0)
+        candidate_sum(3, 0)
+        both(finish, 2)
+        gated_state(3, 1)
+        candidate_product(3, 1)
+        candidate_sum(3, 1)
+        both(finish, 3)

@@ -27,7 +27,7 @@ WORDS = K // 2
 RUN = 8
 VECTOR_SHARE = (5, 8)
 
-IDLE_HEAD = 4
+IDLE_HEAD = 5
 IDLE_LOADS = 2
 
 FLOPS = 4 * 2 * BATCH * K * UNITS
@@ -98,24 +98,34 @@ def tile_augru_pa_kernel(
         bias_square = const.tile([P, P], F32)
         nc.gpsimd.tensor_copy(out=bias_square[:], in_=bias_rows[:])
 
-        def transpose_rows(rows_raw):
+        def transpose_rows(rows_raw, parts=1):
             words = rows_raw[:].bitcast(F32)
-            bank = banks.tile([P, BANK], F32, tag="bank")
-            for t in range(ROW_TILES):
-                for u in range(2):
-                    nc.tensor.transpose(
-                        out=bank[:, u * CHUNK + t * P : u * CHUNK + (t + 1) * P],
-                        in_=words[:, t * WORDS + u : (t + 1) * WORDS : 2],
-                        identity=ident[:],
-                    )
-            return bank
+            row_tiles = ROW_TILES // parts
+            part_banks = []
+            for part in range(parts):
+                bank = banks.tile([P, BANK], F32, tag="bank")
+                for local in range(row_tiles):
+                    t = part * row_tiles + local
+                    for u in range(2):
+                        nc.tensor.transpose(
+                            out=bank[:, (u * row_tiles + local) * P : (u * row_tiles + local + 1) * P],
+                            in_=words[:, t * WORDS + u : (t + 1) * WORDS : 2],
+                            identity=ident[:],
+                        )
+                part_banks.append(bank)
+            return part_banks
 
-        def group_rows(name, bank):
+        def group_rows(name, part_banks):
             grouped = mx.tile([P, CHUNK * PACK], BF16, name=name, align_bytes=64)
-            nc.scalar.copy(
-                out=grouped[:].bitcast(F32).rearrange("q (col u) -> q col u", u=2),
-                in_=bank[:].rearrange("q (u col) -> q col u", u=2),
-            )
+            dst = grouped[:].bitcast(F32)
+            width = 2 * CHUNK // len(part_banks)
+            for part, bank in enumerate(part_banks):
+                nc.scalar.copy(
+                    out=dst[:, part * width : (part + 1) * width].rearrange(
+                        "q (col u) -> q col u", u=2
+                    ),
+                    in_=bank[:, 0:width].rearrange("q (u col) -> q col u", u=2),
+                )
             return grouped[:]
 
         def regroup_weight(name, weight_raw, first=0, pairs=PAIRS):
@@ -187,9 +197,15 @@ def tile_augru_pa_kernel(
 
         def gated_state(c, j):
             product = work.tile([P, BANK], F32, tag="gated")
-            nc.vector.tensor_tensor(
-                out=product[:], in0=gate[c][j][:], in1=state_bank[c][j][:], op=ALU.mult
-            )
+            parts = PAIR if c == N_CHUNKS - 1 else 1
+            for part in range(parts):
+                cols = slice(part * BANK // parts, (part + 1) * BANK // parts)
+                nc.vector.tensor_tensor(
+                    out=product[:, cols],
+                    in0=gate[c][j][:, cols],
+                    in1=state_bank[c][j][:, cols],
+                    op=ALU.mult,
+                )
             gated[c][j] = product
 
         def candidate_product(c, j):
@@ -214,28 +230,28 @@ def tile_augru_pa_kernel(
             summed[c][j] = total
 
         def finish(c, j):
-            bank = banks.tile([P, BANK], F32, tag="bank")
-            for m in range(PAIR):
-                for t in range(ROW_TILES):
-                    nc.tensor.transpose(
-                        out=bank[:, (t * PAIR + m) * P : (t * PAIR + m + 1) * P],
-                        in_=summed[c][j][:, m * CHUNK + t * P : m * CHUNK + (t + 1) * P],
-                        identity=ident[:],
-                    )
-            result = work.tile([P, BANK], F32, tag="result")
-            turned = bank[:].rearrange("p (t n) -> p t n", t=ROW_TILES)
-            stored = result[:].rearrange("p (t n) -> p t n", t=ROW_TILES)
             parts = PAIR if c == N_CHUNKS - 1 and j == PAIRS - 1 else 1
-            width = PAIR * P // parts
+            tiles = PAIR // parts
+            result = work.tile([P, BANK], F32, tag="result")
             for part in range(parts):
-                cols = slice(part * width, (part + 1) * width)
-                first = j * PAIR * P + part * width
-                nc.scalar.activation(out=stored[:, :, cols], in_=turned[:, :, cols], func=ACT.Tanh)
+                bank = banks.tile([P, BANK], F32, tag="bank")
+                for local in range(tiles):
+                    m = part * tiles + local
+                    for t in range(ROW_TILES):
+                        nc.tensor.transpose(
+                            out=bank[:, (t * tiles + local) * P : (t * tiles + local + 1) * P],
+                            in_=summed[c][j][:, m * CHUNK + t * P : m * CHUNK + (t + 1) * P],
+                            identity=ident[:],
+                        )
+                width = ROW_TILES * tiles * P
+                stored = result[:, part * width : (part + 1) * width]
+                nc.scalar.activation(out=stored, in_=bank[:, 0:width], func=ACT.Tanh)
+                first = (j * PAIR + part * tiles) * P
                 nc.sync.dma_start(
-                    out=out[c * CHUNK : (c + 1) * CHUNK, first : first + width].rearrange(
+                    out=out[c * CHUNK : (c + 1) * CHUNK, first : first + tiles * P].rearrange(
                         "(p t) n -> p t n", t=ROW_TILES
                     ),
-                    in_=stored[:, :, cols],
+                    in_=stored.rearrange("p (t n) -> p t n", t=ROW_TILES),
                 )
 
         def both(step, c):
@@ -244,10 +260,10 @@ def tile_augru_pa_kernel(
 
         keep_clock(IDLE_HEAD)
         wxr_grouped = regroup_weight("wxr_grouped", wxr_raw)
-        x_bank = transpose_rows(x_raw[0])
+        x_bank = transpose_rows(x_raw[0], parts=ROW_TILES)
         x_grouped = group_rows("x_grouped0", x_bank)
         wxr = quantise_weight("wxr", wxr_grouped)
-        h_bank = transpose_rows(h_raw[0])
+        h_bank = transpose_rows(h_raw[0], parts=ROW_TILES)
         h_grouped = group_rows("h_grouped0", h_bank)
         bias_bank = banks.tile([P, BANK], F32, tag="bank")
         nc.tensor.transpose(out=bias_bank[:, 0:P], in_=bias_square[:], identity=ident[:])

from contextlib import ExitStack

import concourse.mybir as mybir
from concourse.masks import make_identity

F32 = mybir.dt.float32
BF16 = mybir.dt.bfloat16
U32 = mybir.dt.uint32
U8 = mybir.dt.uint8
FP8X4 = mybir.dt.float8_e4m3fn_x4
ACT = mybir.ActivationFunctionType
ALU = mybir.AluOpType

P = 128
PACK = 4
K = P * PACK
BATCH = 1024
UNITS = 512
CHUNK = 256
N_CHUNKS = BATCH // CHUNK
ROW_TILES = CHUNK // P
UNIT_TILES = UNITS // P
PAIR = 2
PAIRS = UNIT_TILES // PAIR
BANK = PAIR * CHUNK
WORDS = K // 2
RUN = 8
VECTOR_SHARE = (5, 8)

IDLE_HEAD = 5
IDLE_LOADS = 2

FLOPS = 4 * 2 * BATCH * K * UNITS


def tile_augru_pa_kernel(
    tc, input_x, input_h, Wx_r, b_r, Wh_r, Wx_h, b_h, Wh_h, out
):
    nc = tc.nc
    with ExitStack() as ctx:
        const = ctx.enter_context(tc.tile_pool(name="const", bufs=1))
        raw = ctx.enter_context(tc.tile_pool(name="raw", bufs=1))
        mx = ctx.enter_context(tc.tile_pool(name="mx", bufs=1))
        work = ctx.enter_context(tc.tile_pool(name="work", bufs=N_CHUNKS * PAIRS))
        banks = ctx.enter_context(tc.psum_pool(name="banks", bufs=8))
        ctx.enter_context(tc.manual_schedule())

        bias_rows = const.tile([P, P], BF16)
        nc.gpsimd.memset(bias_rows[:], 0.0)
        warm = const.tile([P, 2], F32)
        nc.gpsimd.memset(warm[:], 0.0)
        nc.scalar.activation(out=warm[:, 1:2], in_=warm[:, 0:1], func=ACT.Sigmoid)
        ident = const.tile([P, P], F32)
        make_identity(nc, ident[:])
        idle_zeros = const.tile([P, BANK], BF16)
        nc.vector.memset(idle_zeros[:], 0.0)
        idle_bank = banks.tile([P, BANK], F32, tag="bank")

        def keep_clock(count):
            for n in range(count):
                nc.tensor.matmul(
                    out=idle_bank[:],
                    lhsT=idle_zeros[:, 0:P],
                    rhs=idle_zeros[:],
                    start=True,
                    stop=True,
                )

        def load_rows(name, tensor, c):
            tile = raw.tile([P, ROW_TILES * K], BF16, name=name)
            rows = tensor[c * CHUNK : (c + 1) * CHUNK, :]
            nc.sync.dma_start(out=tile[:], in_=rows.rearrange("(p t) k -> p (t k)", t=ROW_TILES))
            return tile

        def load_weight(name, weight):
            tile = raw.tile([P, PACK, UNITS], BF16, name=name)
            nc.sync.dma_start(out=tile[:], in_=weight.rearrange("(q j) n -> q j n", j=PACK))
            return tile

        x_raw = [None] * N_CHUNKS
        h_raw = [None] * N_CHUNKS
        wxr_raw = load_weight("wxr_raw", Wx_r)
        x_raw[0] = load_rows("x_raw0", input_x, 0)
        h_raw[0] = load_rows("h_raw0", input_h, 0)
        nc.sync.dma_start(out=bias_rows[0:UNIT_TILES, :], in_=b_r.rearrange("(i n) -> i n", n=P))
        nc.sync.dma_start(
            out=bias_rows[UNIT_TILES : 2 * UNIT_TILES, :], in_=b_h.rearrange("(i n) -> i n", n=P)
        )
        whr_raw = load_weight("whr_raw", Wh_r)
        x_raw[1] = load_rows("x_raw1", input_x, 1)
        whh_raw = load_weight("whh_raw", Wh_h)
        h_raw[1] = load_rows("h_raw1", input_h, 1)
        x_raw[2] = load_rows("x_raw2", input_x, 2)
        wxh_raw = load_weight("wxh_raw", Wx_h)
        h_raw[2] = load_rows("h_raw2", input_h, 2)
        x_raw[3] = load_rows("x_raw3", input_x, 3)
        h_raw[3] = load_rows("h_raw3", input_h, 3)
        bias_square = const.tile([P, P], F32)
        nc.gpsimd.tensor_copy(out=bias_square[:], in_=bias_rows[:])

        def transpose_rows(rows_raw, parts=1):
            words = rows_raw[:].bitcast(F32)
            row_tiles = ROW_TILES // parts
            part_banks = []
            for part in range(parts):
                bank = banks.tile([P, BANK], F32, tag="bank")
                for local in range(row_tiles):
                    t = part * row_tiles + local
                    for u in range(2):
                        nc.tensor.transpose(
                            out=bank[:, (u * row_tiles + local) * P : (u * row_tiles + local + 1) * P],
                            in_=words[:, t * WORDS + u : (t + 1) * WORDS : 2],
                            identity=ident[:],
                        )
                part_banks.append(bank)
            return part_banks

        def group_rows(name, part_banks):
            grouped = mx.tile([P, CHUNK * PACK], BF16, name=name, align_bytes=64)
            dst = grouped[:].bitcast(F32)
            width = 2 * CHUNK // len(part_banks)
            for part, bank in enumerate(part_banks):
                nc.scalar.copy(
                    out=dst[:, part * width : (part + 1) * width].rearrange(
                        "q (col u) -> q col u", u=2
                    ),
                    in_=bank[:, 0:width].rearrange("q (u col) -> q col u", u=2),
                )
            return grouped[:]

        def regroup_weight(name, weight_raw, first=0, pairs=PAIRS):
            units = pairs * PAIR * P
            grouped = mx.tile([P, units, PACK], BF16, name=name, align_bytes=64)
            raw_units = weight_raw[:, :, first * PAIR * P : first * PAIR * P + units]
            dst = grouped[:].rearrange("q (c i) t -> q c t i", i=RUN)
            src = raw_units.rearrange("q t (c i) -> q c t i", i=RUN)
            cut = units // RUN * VECTOR_SHARE[0] // VECTOR_SHARE[1]
            nc.vector.tensor_copy(out=dst[:, :cut], in_=src[:, :cut])
            nc.scalar.copy(out=dst[:, cut:], in_=src[:, cut:])
            return grouped[:].rearrange("q n t -> q (n t)")

        def quantise(name, grouped, columns):
            codes = mx.tile([P, columns], U32, name=name + "_codes", align_bytes=256)
            scales = mx.tile([P, columns], U8, name=name + "_scales", align_bytes=256)
            nc.vector.quantize_mx(out=codes[:].bitcast(FP8X4), scales=scales[:], in_=grouped)
            return codes, scales

        def quantise_weight(name, grouped, pairs=PAIRS):
            codes, scales = quantise(name, grouped, pairs * PAIR * P)
            width = PAIR * P
            return [
                (codes[:, j * width : (j + 1) * width], scales[:, j * width : (j + 1) * width])
                for j in range(pairs)
            ]

        def mx_pass(acc, m, weight, rows, start, stop):
            units = slice(m * P, (m + 1) * P)
            nc.tensor.matmul_mx(
                out=acc[:, m * CHUNK : (m + 1) * CHUNK],
                lhsT=weight[0][:, units].bitcast(FP8X4),
                lhsT_scale=weight[1][:, units],
                rhs=rows[0][:].bitcast(FP8X4),
                rhs_scale=rows[1][:],
                start=start,
                stop=stop,
            )

        x_mx = [None] * N_CHUNKS
        h_mx = [None] * N_CHUNKS
        gate = [[None] * PAIRS for c in range(N_CHUNKS)]
        state_bank = [[None] * PAIRS for c in range(N_CHUNKS)]
        gated = [[None] * PAIRS for c in range(N_CHUNKS)]
        candidate_bank = [[None] * PAIRS for c in range(N_CHUNKS)]
        summed = [[None] * PAIRS for c in range(N_CHUNKS)]

        def reset_gate(c, j):
            acc = banks.tile([P, BANK], F32, tag="bank")
            for m in range(PAIR):
                mx_pass(acc, m, wxr[j], x_mx[c], True, False)
                mx_pass(acc, m, whr[j], h_mx[c], False, True)
            r = work.tile([P, BANK], F32, tag="gate")
            for m in range(PAIR):
                i = j * PAIR + m
                nc.scalar.activation(
                    out=r[:, m * CHUNK : (m + 1) * CHUNK],
                    in_=acc[:, m * CHUNK : (m + 1) * CHUNK],
                    func=ACT.Sigmoid,
                    bias=bias[:, i : i + 1],
                )
            gate[c][j] = r

        def state_product(c, j):
            acc = banks.tile([P, BANK], F32, tag="bank")
            for m in range(PAIR):
                mx_pass(acc, m, whh[j], h_mx[c], True, True)
            state_bank[c][j] = acc

        def gated_state(c, j):
            product = work.tile([P, BANK], F32, tag="gated")
            parts = PAIR if c == N_CHUNKS - 1 else 1
            for part in range(parts):
                cols = slice(part * BANK // parts, (part + 1) * BANK // parts)
                nc.vector.tensor_tensor(
                    out=product[:, cols],
                    in0=gate[c][j][:, cols],
                    in1=state_bank[c][j][:, cols],
                    op=ALU.mult,
                )
            gated[c][j] = product

        def candidate_product(c, j):
            acc = banks.tile([P, BANK], F32, tag="bank")
            for m in range(PAIR):
                mx_pass(acc, m, wxh[j], x_mx[c], True, True)
            candidate_bank[c][j] = acc

        def candidate_sum(c, j):
            acc = candidate_bank[c][j]
            total = work.tile([P, BANK], F32, tag="summed")
            for m in range(PAIR):
                i = UNIT_TILES + j * PAIR + m
                nc.vector.scalar_tensor_tensor(
                    out=total[:, m * CHUNK : (m + 1) * CHUNK],
                    in0=acc[:, m * CHUNK : (m + 1) * CHUNK],
                    scalar=bias[:, i : i + 1],
                    in1=gated[c][j][:, m * CHUNK : (m + 1) * CHUNK],
                    op0=ALU.add,
                    op1=ALU.add,
                )
            summed[c][j] = total

        def finish(c, j):
            parts = PAIR if c == N_CHUNKS - 1 and j == PAIRS - 1 else 1
            tiles = PAIR // parts
            result = work.tile([P, BANK], F32, tag="result")
            for part in range(parts):
                bank = banks.tile([P, BANK], F32, tag="bank")
                for local in range(tiles):
                    m = part * tiles + local
                    for t in range(ROW_TILES):
                        nc.tensor.transpose(
                            out=bank[:, (t * tiles + local) * P : (t * tiles + local + 1) * P],
                            in_=summed[c][j][:, m * CHUNK + t * P : m * CHUNK + (t + 1) * P],
                            identity=ident[:],
                        )
                width = ROW_TILES * tiles * P
                stored = result[:, part * width : (part + 1) * width]
                nc.scalar.activation(out=stored, in_=bank[:, 0:width], func=ACT.Tanh)
                first = (j * PAIR + part * tiles) * P
                nc.sync.dma_start(
                    out=out[c * CHUNK : (c + 1) * CHUNK, first : first + tiles * P].rearrange(
                        "(p t) n -> p t n", t=ROW_TILES
                    ),
                    in_=stored.rearrange("p (t n) -> p t n", t=ROW_TILES),
                )

        def both(step, c):
            for j in range(PAIRS):
                step(c, j)

        keep_clock(IDLE_HEAD)
        wxr_grouped = regroup_weight("wxr_grouped", wxr_raw)
        x_bank = transpose_rows(x_raw[0], parts=ROW_TILES)
        x_grouped = group_rows("x_grouped0", x_bank)
        wxr = quantise_weight("wxr", wxr_grouped)
        h_bank = transpose_rows(h_raw[0], parts=ROW_TILES)
        h_grouped = group_rows("h_grouped0", h_bank)
        bias_bank = banks.tile([P, BANK], F32, tag="bank")
        nc.tensor.transpose(out=bias_bank[:, 0:P], in_=bias_square[:], identity=ident[:])
        keep_clock(IDLE_LOADS)
        x_mx[0] = quantise("x0", x_grouped, CHUNK)
        whr_grouped = [regroup_weight("whr_grouped%d" % j, whr_raw, j, 1) for j in range(PAIRS)]
        h_mx[0] = quantise("h0", h_grouped, CHUNK)
        whr = quantise_weight("whr0", whr_grouped[0], 1)
        bias = const.tile([P, 2 * UNIT_TILES], F32)
        nc.vector.tensor_copy(out=bias[:], in_=bias_bank[:, 0 : 2 * UNIT_TILES])
        whr = whr + quantise_weight("whr1", whr_grouped[1], 1)
        x_bank = transpose_rows(x_raw[1])
        x_grouped = group_rows("x_grouped1", x_bank)
        whh_grouped = [regroup_weight("whh_grouped%d" % j, whh_raw, j, 1) for j in range(PAIRS)]
        both(reset_gate, 0)
        x_mx[1] = quantise("x1", x_grouped, CHUNK)
        whh = quantise_weight("whh0", whh_grouped[0], 1)
        whh = whh + quantise_weight("whh1", whh_grouped[1], 1)
        h_bank = transpose_rows(h_raw[1])
        h_grouped = group_rows("h_grouped1", h_bank)
        wxh_grouped = regroup_weight("wxh_grouped", wxh_raw)
        x_bank = transpose_rows(x_raw[2])
        x_grouped = group_rows("x_grouped2", x_bank)
        both(state_product, 0)
        h_mx[1] = quantise("h1", h_grouped, CHUNK)
        gated_state(0, 0)
        wxh = quantise_weight("wxh", wxh_grouped)
        gated_state(0, 1)
        h_bank = transpose_rows(h_raw[2])
        both(reset_gate, 1)
        h_grouped = group_rows("h_grouped2", h_bank)
        x_mx[2] = quantise("x2", x_grouped, CHUNK)
        both(candidate_product, 0)
        both(candidate_sum, 0)
        both(state_product, 1)
        h_mx[2] = quantise("h2", h_grouped, CHUNK)
        both(gated_state, 1)
        x_bank = transpose_rows(x_raw[3])
        x_grouped = group_rows("x_grouped3", x_bank)
        h_bank = transpose_rows(h_raw[3])
        h_grouped = group_rows("h_grouped3", h_bank)
        both(finish, 0)
        x_mx[3] = quantise("x3", x_grouped, CHUNK)
        both(candidate_product, 1)
        both(candidate_sum, 1)
        h_mx[3] = quantise("h3", h_grouped, CHUNK)
        both(reset_gate, 2)
        both(state_product, 2)
        both(gated_state, 2)
        both(finish, 1)
        candidate_product(2, 0)
        reset_gate(3, 0)
        candidate_product(2, 1)
        both(candidate_sum, 2)
        state_product(3, 0)
        gated_state(3, 0)
        reset_gate(3, 1)
        state_product(3, 1)
        candidate_product(3, 0)
        candidate_sum(3, 0)
        both(finish, 2)
        gated_state(3, 1)
        candidate_product(3, 1)
        candidate_sum(3, 1)
        both(finish, 3)
